import numpy as np
import ml_dtypes

BF16 = ml_dtypes.bfloat16


def bf(x):
    return np.asarray(x, np.float32).astype(BF16)


def f32(x):
    return np.asarray(x, np.float32)


def f64(x):
    return np.asarray(x).astype(np.float64)


def striped(idx):
    return np.tile(idx.reshape(-1, 16).T, (8, 1))


NN, R, CIN, KC, C, S, N = 128, 8, 1024, 3, 512, 2048, 1024
DENS, FLOOR = 0.125, 0.01


def lap(adj):
    a = adj * (1.0 - np.eye(NN))
    d0 = 1.0 / np.sqrt(a.sum(0))
    d1 = 1.0 / np.sqrt(a.sum(1))
    return d0[:, None] * a * d1[None, :]


def setup_inputs():
    x = bf(np.random.standard_normal((CIN, N)))
    adj = f32(FLOOR + np.random.uniform(size=(NN, NN)) * (np.random.uniform(size=(NN, NN)) < DENS) + np.eye(NN))
    w = bf(np.random.standard_normal((KC * CIN, C)) / np.sqrt(CIN))
    b = f32(0.3 * np.random.standard_normal((C, 1)))
    base = f32(np.random.standard_normal((C, S)))
    return {"x": x, "adj": adj, "w": w, "b": b, "base": base, "offs": striped(np.random.permutation(S)[:N])}


def reference(x, adj, w, b, base, offs):
    idx = offs[:16].T.reshape(-1)
    lp = lap(f64(adj))
    t0 = f64(x).reshape(CIN, R, NN)
    t1 = np.einsum('en,drn->dre', lp, t0)
    t2 = 2.0 * np.einsum('en,drn->dre', lp, t1) - t0
    tx = np.concatenate([t0, t1, t2], axis=0).reshape(KC * CIN, N)
    out = f64(base).copy()
    out[:, idx] = f64(w).T @ tx + f64(b)
    return out

@@ -1,0 +1,134 @@
+import concourse.mybir as mybir
+from concourse.masks import make_identity
+
+BF16, F32, U16 = mybir.dt.bfloat16, mybir.dt.float32, mybir.dt.uint16
+ADD, MULT, SUBTRACT = mybir.AluOpType.add, mybir.AluOpType.mult, mybir.AluOpType.subtract
+
+P = 128
+ROWS = 8
+N = ROWS * P
+C_IN, ORDERS, C_OUT, STORE = 1024, 3, 512, 2048
+IN_BLOCKS = C_IN // P
+OUT_BLOCKS = C_OUT // P
+BANK = 512
+HALVES = N // BANK
+ROWS_PER_BANK = BANK // P
+
+FLOPS = 2 * ORDERS * C_IN * C_OUT * N + 2 * (2 * P * P * C_IN * ROWS)
+
+
+def tile_chebconv2d_b_kernel(tc, x, adj, w, b, base, offs, out):
+    nc = tc.nc
+    with (
+        tc.tile_pool(name="held", bufs=1) as held,
+        tc.tile_pool(name="turned", bufs=3) as turned,
+        tc.tile_pool(name="dense", bufs=2) as dense,
+        tc.psum_pool(name="psum_y", bufs=3) as psum_y,
+        tc.psum_pool(name="psum_bf16", bufs=3) as psum_bf16,
+        tc.psum_pool(name="psum_f32", bufs=2) as psum_f32,
+    ):
+        adj_sb = held.tile([P, P], F32, name="adj_sb")
+        nc.sync.dma_start(adj_sb[:], adj)
+        x_sb = [held.tile([P, N], BF16, name=f"x{i}") for i in range(IN_BLOCKS)]
+        for i in range(IN_BLOCKS):
+            nc.sync.dma_start(x_sb[i][:], x[i * P : (i + 1) * P, :])
+        w_sb = [held.tile([P, IN_BLOCKS, C_OUT], BF16, name=f"w{k}") for k in range(ORDERS)]
+        for k in range(ORDERS):
+            rows_of_order = w[k * C_IN : (k + 1) * C_IN, :]
+            nc.sync.dma_start(w_sb[k][:], rows_of_order.rearrange("(i p) c -> p i c", p=P))
+        offsets = held.tile([P, N // 16], U16, name="offsets")
+        nc.sync.dma_start(offsets[:], offs)
+        bias = held.tile([P, OUT_BLOCKS], F32, name="bias")
+        with nc.allow_non_contiguous_dma(reason="512 floats, one to a partition and block"):
+            nc.sync.dma_start(bias[:], b.rearrange("(o p) one -> p (o one)", p=P))
+        window = [held.tile([P, STORE], F32, name=f"window{o}") for o in range(OUT_BLOCKS)]
+        for o in range(OUT_BLOCKS):
+            nc.sync.dma_start(window[o][:], base[o * P : (o + 1) * P, :])
+        bias_wide = [held.tile([P, N], F32, name=f"bias_wide{o}") for o in range(OUT_BLOCKS)]
+        for o in range(OUT_BLOCKS):
+            nc.gpsimd.tensor_copy(bias_wide[o][:], bias[:, o : o + 1].to_broadcast([P, N]))
+
+        identity_f32 = held.tile([P, P], F32, name="identity_f32")
+        make_identity(nc, identity_f32[:])
+        identity_bf16 = held.tile([P, P], BF16, name="identity_bf16")
+        make_identity(nc, identity_bf16[:])
+        ones = held.tile([P, 1], F32, name="ones")
+        nc.vector.memset(ones[:], 1.0)
+
+        off_diagonal = held.tile([P, P], F32, name="off_diagonal")
+        nc.vector.tensor_scalar(off_diagonal[:], identity_f32[:], -1.0, 1.0, op0=MULT, op1=ADD)
+        a_sb = held.tile([P, P], F32, name="a_sb")
+        nc.vector.tensor_tensor(a_sb[:], adj_sb[:], off_diagonal[:], MULT)
+        row_sums = held.tile([P, 1], F32, name="row_sums")
+        nc.vector.reduce_sum(row_sums[:], a_sb[:], axis=mybir.AxisListType.X)
+        col_sums = psum_f32.tile([P, BANK], F32, tag="bank", name="col_sums")
+        nc.tensor.matmul(col_sums[:, 0:1], lhsT=a_sb[:], rhs=ones[:], start=True, stop=True)
+        roots = held.tile([P, 2], F32, name="roots")
+        nc.scalar.sqrt(roots[:, 0:1], col_sums[:, 0:1])
+        nc.scalar.sqrt(roots[:, 1:2], row_sums[:])
+        inverse_roots = held.tile([P, 2], F32, name="inverse_roots")
+        nc.vector.reciprocal(inverse_roots[:], roots[:])
+        a_scaled = held.tile([P, P], F32, name="a_scaled")
+        nc.vector.tensor_scalar_mul(a_scaled[:], a_sb[:], inverse_roots[:, 0:1])
+        a_turned = psum_f32.tile([P, BANK], F32, tag="bank", name="a_turned")
+        nc.tensor.transpose(a_turned[:, 0:P], a_scaled[:], identity_f32[:])
+        lt = held.tile([P, P], BF16, name="lt")
+        nc.vector.tensor_scalar_mul(lt[:], a_turned[:, 0:P], inverse_roots[:, 1:2])
+
+        t1 = [held.tile([P, N], BF16, name=f"t1_{i}") for i in range(IN_BLOCKS)]
+        t2 = [held.tile([P, N], BF16, name=f"t2_{i}") for i in range(IN_BLOCKS)]
+        for i in range(IN_BLOCKS):
+            xt_ps = psum_bf16.tile([P, N], BF16, tag="bank", name="xt_ps")
+            for r in range(ROWS):
+                row = slice(r * P, (r + 1) * P)
+                nc.tensor.transpose(xt_ps[:, row], x_sb[i][:, row], identity_bf16[:])
+            xt = turned.tile([P, N], BF16, name="xt")
+            nc.vector.tensor_copy(xt[:], xt_ps[:])
+
+            t1t_ps = psum_bf16.tile([P, N], BF16, tag="bank", name="t1t_ps")
+            for h in range(HALVES):
+                half = slice(h * BANK, (h + 1) * BANK)
+                nc.tensor.matmul(t1t_ps[:, half], lhsT=lt[:], rhs=xt[:, half], start=True, stop=True)
+            t1t = turned.tile([P, N], BF16, name="t1t")
+            nc.scalar.copy(t1t[:], t1t_ps[:])
+
+            t1_ps = psum_bf16.tile([P, N], BF16, tag="bank", name="t1_ps")
+            for r in range(ROWS):
+                row = slice(r * P, (r + 1) * P)
+                nc.tensor.matmul(t1_ps[:, row], lhsT=xt[:, row], rhs=lt[:], start=True, stop=True)
+            nc.scalar.copy(t1[i][:], t1_ps[:])
+
+            for h in range(HALVES):
+                half = slice(h * BANK, (h + 1) * BANK)
+                t2_ps = psum_f32.tile([P, BANK], F32, tag="bank", name="t2_ps")
+                for q in range(ROWS_PER_BANK):
+                    r = h * ROWS_PER_BANK + q
+                    nc.tensor.matmul(
+                        t2_ps[:, q * P : (q + 1) * P],
+                        lhsT=t1t[:, r * P : (r + 1) * P],
+                        rhs=lt[:],
+                        start=True,
+                        stop=True,
+                    )
+                nc.vector.scalar_tensor_tensor(
+                    t2[i][:, half], in0=t2_ps[:], scalar=2.0, in1=x_sb[i][:, half], op0=MULT, op1=SUBTRACT
+                )
+
+        terms = [x_sb, t1, t2]
+        for o in range(OUT_BLOCKS):
+            y_sb = dense.tile([P, N], F32, name="y_sb")
+            for h in range(HALVES):
+                half = slice(h * BANK, (h + 1) * BANK)
+                y_ps = psum_y.tile([P, BANK], F32, name="y_ps")
+                for k in range(ORDERS):
+                    for i in range(IN_BLOCKS):
+                        nc.tensor.matmul(
+                            y_ps[:],
+                            lhsT=w_sb[k][:, i, o * P : (o + 1) * P],
+                            rhs=terms[k][i][:, half],
+                            start=(k == 0 and i == 0),
+                            stop=(k == ORDERS - 1 and i == IN_BLOCKS - 1),
+                        )
+                nc.scalar.copy(y_sb[:, half], y_ps[:])
+            nc.vector.tensor_tensor(window[o][:].indirect(offsets[:]), y_sb[:], bias_wide[o][:], ADD)
+            nc.sync.dma_start(out[o * P : (o + 1) * P, :], window[o][:])

@@ -21,7 +21,7 @@ def tile_chebconv2d_b_kernel(tc, x, adj, w, b, base, offs, out):
     nc = tc.nc
     with (
         tc.tile_pool(name="held", bufs=1) as held,
-        tc.tile_pool(name="turned", bufs=3) as turned,
+        tc.tile_pool(name="turned", bufs=IN_BLOCKS) as turned,
         tc.tile_pool(name="dense", bufs=2) as dense,
         tc.psum_pool(name="psum_y", bufs=3) as psum_y,
         tc.psum_pool(name="psum_bf16", bufs=3) as psum_bf16,
@@ -30,10 +30,11 @@ def tile_chebconv2d_b_kernel(tc, x, adj, w, b, base, offs, out):
         adj_sb = held.tile([P, P], F32, name="adj_sb")
         nc.sync.dma_start(adj_sb[:], adj)
         x_sb = [held.tile([P, N], BF16, name=f"x{i}") for i in range(IN_BLOCKS)]
+        w_sb = [held.tile([P, IN_BLOCKS, C_OUT], BF16, name=f"w{k}") for k in range(ORDERS)]
         for i in range(IN_BLOCKS):
             nc.sync.dma_start(x_sb[i][:], x[i * P : (i + 1) * P, :])
-        w_sb = [held.tile([P, IN_BLOCKS, C_OUT], BF16, name=f"w{k}") for k in range(ORDERS)]
-        for k in range(ORDERS):
+            nc.sync.dma_start(w_sb[0][:, i, :], w[i * P : (i + 1) * P, :])
+        for k in range(1, ORDERS):
             rows_of_order = w[k * C_IN : (k + 1) * C_IN, :]
             nc.sync.dma_start(w_sb[k][:], rows_of_order.rearrange("(i p) c -> p i c", p=P))
         offsets = held.tile([P, N // 16], U16, name="offsets")

@@ -13,6 +13,7 @@ OUT_BLOCKS = C_OUT // P
 BANK = 512
 HALVES = N // BANK
 ROWS_PER_BANK = BANK // P
+WARM_UP = 5
 
 FLOPS = 2 * ORDERS * C_IN * C_OUT * N + 2 * (2 * P * P * C_IN * ROWS)
 
@@ -48,6 +49,12 @@ def tile_chebconv2d_b_kernel(tc, x, adj, w, b, base, offs, out):
         bias_wide = [held.tile([P, N], F32, name=f"bias_wide{o}") for o in range(OUT_BLOCKS)]
         for o in range(OUT_BLOCKS):
             nc.gpsimd.tensor_copy(bias_wide[o][:], bias[:, o : o + 1].to_broadcast([P, N]))
+
+        zeros = held.tile([P, BANK], BF16, name="zeros")
+        nc.vector.memset(zeros[:], 0.0)
+        warm_ps = psum_f32.tile([P, BANK], F32, tag="bank", name="warm_ps")
+        for repeat in range(WARM_UP):
+            nc.tensor.matmul(warm_ps[:], lhsT=zeros[:, 0:P], rhs=zeros[:], start=True, stop=True)
 
         identity_f32 = held.tile([P, P], F32, name="identity_f32")
         make_identity(nc, identity_f32[:])

@@ -11,8 +11,11 @@ C_IN, ORDERS, C_OUT, STORE = 1024, 3, 512, 2048
 IN_BLOCKS = C_IN // P
 OUT_BLOCKS = C_OUT // P
 BANK = 512
+BANKS = 8
 HALVES = N // BANK
 ROWS_PER_BANK = BANK // P
+EARLY_OUT_BLOCKS = 2
+STAGES = 3
 WARM_UP = 5
 
 FLOPS = 2 * ORDERS * C_IN * C_OUT * N + 2 * (2 * P * P * C_IN * ROWS)
@@ -22,11 +25,8 @@ def tile_chebconv2d_b_kernel(tc, x, adj, w, b, base, offs, out):
     nc = tc.nc
     with (
         tc.tile_pool(name="held", bufs=1) as held,
-        tc.tile_pool(name="turned", bufs=IN_BLOCKS) as turned,
         tc.tile_pool(name="dense", bufs=2) as dense,
-        tc.psum_pool(name="psum_y", bufs=3) as psum_y,
-        tc.psum_pool(name="psum_bf16", bufs=3) as psum_bf16,
-        tc.psum_pool(name="psum_f32", bufs=2) as psum_f32,
+        tc.psum_pool(name="psum", bufs=BANKS) as psum,
     ):
         adj_sb = held.tile([P, P], F32, name="adj_sb")
         nc.sync.dma_start(adj_sb[:], adj)
@@ -34,10 +34,9 @@ def tile_chebconv2d_b_kernel(tc, x, adj, w, b, base, offs, out):
         w_sb = [held.tile([P, IN_BLOCKS, C_OUT], BF16, name=f"w{k}") for k in range(ORDERS)]
         for i in range(IN_BLOCKS):
             nc.sync.dma_start(x_sb[i][:], x[i * P : (i + 1) * P, :])
-            nc.sync.dma_start(w_sb[0][:, i, :], w[i * P : (i + 1) * P, :])
-        for k in range(1, ORDERS):
-            rows_of_order = w[k * C_IN : (k + 1) * C_IN, :]
-            nc.sync.dma_start(w_sb[k][:], rows_of_order.rearrange("(i p) c -> p i c", p=P))
+            for k in range(ORDERS):
+                first_row = k * C_IN + i * P
+                nc.sync.dma_start(w_sb[k][:, i, :], w[first_row : first_row + P, :])
         offsets = held.tile([P, N // 16], U16, name="offsets")
         nc.sync.dma_start(offsets[:], offs)
         bias = held.tile([P, OUT_BLOCKS], F32, name="bias")
@@ -52,7 +51,7 @@ def tile_chebconv2d_b_kernel(tc, x, adj, w, b, base, offs, out):
 
         zeros = held.tile([P, BANK], BF16, name="zeros")
         nc.vector.memset(zeros[:], 0.0)
-        warm_ps = psum_f32.tile([P, BANK], F32, tag="bank", name="warm_ps")
+        warm_ps = psum.tile([P, BANK], F32, tag="bank", name="warm_ps")
         for repeat in range(WARM_UP):
             nc.tensor.matmul(warm_ps[:], lhsT=zeros[:, 0:P], rhs=zeros[:], start=True, stop=True)
 
@@ -69,7 +68,7 @@ def tile_chebconv2d_b_kernel(tc, x, adj, w, b, base, offs, out):
         nc.vector.tensor_tensor(a_sb[:], adj_sb[:], off_diagonal[:], MULT)
         row_sums = held.tile([P, 1], F32, name="row_sums")
         nc.vector.reduce_sum(row_sums[:], a_sb[:], axis=mybir.AxisListType.X)
-        col_sums = psum_f32.tile([P, BANK], F32, tag="bank", name="col_sums")
+        col_sums = psum.tile([P, BANK], F32, tag="bank", name="col_sums")
         nc.tensor.matmul(col_sums[:, 0:1], lhsT=a_sb[:], rhs=ones[:], start=True, stop=True)
         roots = held.tile([P, 2], F32, name="roots")
         nc.scalar.sqrt(roots[:, 0:1], col_sums[:, 0:1])
@@ -78,42 +77,45 @@ def tile_chebconv2d_b_kernel(tc, x, adj, w, b, base, offs, out):
         nc.vector.reciprocal(inverse_roots[:], roots[:])
         a_scaled = held.tile([P, P], F32, name="a_scaled")
         nc.vector.tensor_scalar_mul(a_scaled[:], a_sb[:], inverse_roots[:, 0:1])
-        a_turned = psum_f32.tile([P, BANK], F32, tag="bank", name="a_turned")
+        a_turned = psum.tile([P, BANK], F32, tag="bank", name="a_turned")
         nc.tensor.transpose(a_turned[:, 0:P], a_scaled[:], identity_f32[:])
         lt = held.tile([P, P], BF16, name="lt")
         nc.vector.tensor_scalar_mul(lt[:], a_turned[:, 0:P], inverse_roots[:, 1:2])
 
+        xt = [held.tile([P, N], BF16, name=f"xt{i}") for i in range(IN_BLOCKS)]
+        t1t = [held.tile([P, N], BF16, name=f"t1t{i}") for i in range(IN_BLOCKS)]
         t1 = [held.tile([P, N], BF16, name=f"t1_{i}") for i in range(IN_BLOCKS)]
         t2 = [held.tile([P, N], BF16, name=f"t2_{i}") for i in range(IN_BLOCKS)]
-        for i in range(IN_BLOCKS):
-            xt_ps = psum_bf16.tile([P, N], BF16, tag="bank", name="xt_ps")
+        terms = [x_sb, t1, t2]
+
+        def turn_x(i):
+            xt_ps = psum.tile([P, N], BF16, tag="bank", name="xt_ps")
             for r in range(ROWS):
                 row = slice(r * P, (r + 1) * P)
                 nc.tensor.transpose(xt_ps[:, row], x_sb[i][:, row], identity_bf16[:])
-            xt = turned.tile([P, N], BF16, name="xt")
-            nc.vector.tensor_copy(xt[:], xt_ps[:])
+            nc.vector.tensor_copy(xt[i][:], xt_ps[:])
 
-            t1t_ps = psum_bf16.tile([P, N], BF16, tag="bank", name="t1t_ps")
+        def first_order(i):
+            t1t_ps = psum.tile([P, N], BF16, tag="bank", name="t1t_ps")
             for h in range(HALVES):
                 half = slice(h * BANK, (h + 1) * BANK)
-                nc.tensor.matmul(t1t_ps[:, half], lhsT=lt[:], rhs=xt[:, half], start=True, stop=True)
-            t1t = turned.tile([P, N], BF16, name="t1t")
-            nc.scalar.copy(t1t[:], t1t_ps[:])
-
-            t1_ps = psum_bf16.tile([P, N], BF16, tag="bank", name="t1_ps")
+                nc.tensor.matmul(t1t_ps[:, half], lhsT=lt[:], rhs=xt[i][:, half], start=True, stop=True)
+            nc.scalar.copy(t1t[i][:], t1t_ps[:])
+            t1_ps = psum.tile([P, N], BF16, tag="bank", name="t1_ps")
             for r in range(ROWS):
                 row = slice(r * P, (r + 1) * P)
-                nc.tensor.matmul(t1_ps[:, row], lhsT=xt[:, row], rhs=lt[:], start=True, stop=True)
+                nc.tensor.matmul(t1_ps[:, row], lhsT=xt[i][:, row], rhs=lt[:], start=True, stop=True)
             nc.scalar.copy(t1[i][:], t1_ps[:])
 
+        def second_order(i):
             for h in range(HALVES):
                 half = slice(h * BANK, (h + 1) * BANK)
-                t2_ps = psum_f32.tile([P, BANK], F32, tag="bank", name="t2_ps")
+                t2_ps = psum.tile([P, BANK], F32, tag="bank", name="t2_ps")
                 for q in range(ROWS_PER_BANK):
                     r = h * ROWS_PER_BANK + q
                     nc.tensor.matmul(
                         t2_ps[:, q * P : (q + 1) * P],
-                        lhsT=t1t[:, r * P : (r + 1) * P],
+                        lhsT=t1t[i][:, r * P : (r + 1) * P],
                         rhs=lt[:],
                         start=True,
                         stop=True,
@@ -122,21 +124,52 @@ def tile_chebconv2d_b_kernel(tc, x, adj, w, b, base, offs, out):
                     t2[i][:, half], in0=t2_ps[:], scalar=2.0, in1=x_sb[i][:, half], op0=MULT, op1=SUBTRACT
                 )
 
-        terms = [x_sb, t1, t2]
-        for o in range(OUT_BLOCKS):
+        def add_to_y(y_ps, o, h, k, i):
+            nc.tensor.matmul(
+                y_ps[:],
+                lhsT=w_sb[k][:, i, o * P : (o + 1) * P],
+                rhs=terms[k][i][:, h * BANK : (h + 1) * BANK],
+                start=(k == 0 and i == 0),
+                stop=(k == ORDERS - 1 and i == IN_BLOCKS - 1),
+            )
+
+        def place(o, y_halves):
             y_sb = dense.tile([P, N], F32, name="y_sb")
             for h in range(HALVES):
-                half = slice(h * BANK, (h + 1) * BANK)
-                y_ps = psum_y.tile([P, BANK], F32, name="y_ps")
-                for k in range(ORDERS):
-                    for i in range(IN_BLOCKS):
-                        nc.tensor.matmul(
-                            y_ps[:],
-                            lhsT=w_sb[k][:, i, o * P : (o + 1) * P],
-                            rhs=terms[k][i][:, half],
-                            start=(k == 0 and i == 0),
-                            stop=(k == ORDERS - 1 and i == IN_BLOCKS - 1),
-                        )
-                nc.scalar.copy(y_sb[:, half], y_ps[:])
+                nc.scalar.copy(y_sb[:, h * BANK : (h + 1) * BANK], y_halves[h][:])
             nc.vector.tensor_tensor(window[o][:].indirect(offsets[:]), y_sb[:], bias_wide[o][:], ADD)
             nc.sync.dma_start(out[o * P : (o + 1) * P, :], window[o][:])
+
+        early = [
+            [psum.tile([P, BANK], F32, tag="bank", name=f"y_ps{o}_{h}") for h in range(HALVES)]
+            for o in range(EARLY_OUT_BLOCKS)
+        ]
+
+        def feed_early(k, i):
+            for o in range(EARLY_OUT_BLOCKS):
+                for h in range(HALVES):
+                    add_to_y(early[o][h], o, h, k, i)
+
+        for s in range(IN_BLOCKS + STAGES):
+            if s < IN_BLOCKS:
+                turn_x(s)
+                feed_early(0, s)
+            if 0 <= s - 1 < IN_BLOCKS:
+                first_order(s - 1)
+            if 0 <= s - 2 < IN_BLOCKS:
+                feed_early(1, s - 2)
+                second_order(s - 2)
+            if 0 <= s - 3 < IN_BLOCKS:
+                feed_early(2, s - 3)
+        for o in range(EARLY_OUT_BLOCKS):
+            place(o, early[o])
+
+        for o in range(EARLY_OUT_BLOCKS, OUT_BLOCKS):
+            y_halves = []
+            for h in range(HALVES):
+                y_ps = psum.tile([P, BANK], F32, tag="bank", name="y_ps")
+                for k in range(ORDERS):
+                    for i in range(IN_BLOCKS):
+                        add_to_y(y_ps, o, h, k, i)
+                y_halves.append(y_ps)
+            place(o, y_halves)

@@ -16,6 +16,7 @@ HALVES = N // BANK
 ROWS_PER_BANK = BANK // P
 EARLY_OUT_BLOCKS = 2
 STAGES = 3
+FEED_LAG = (0, 2, 3)
 WARM_UP = 5
 
 FLOPS = 2 * ORDERS * C_IN * C_OUT * N + 2 * (2 * P * P * C_IN * ROWS)
@@ -32,11 +33,14 @@ def tile_chebconv2d_b_kernel(tc, x, adj, w, b, base, offs, out):
         nc.sync.dma_start(adj_sb[:], adj)
         x_sb = [held.tile([P, N], BF16, name=f"x{i}") for i in range(IN_BLOCKS)]
         w_sb = [held.tile([P, IN_BLOCKS, C_OUT], BF16, name=f"w{k}") for k in range(ORDERS)]
-        for i in range(IN_BLOCKS):
-            nc.sync.dma_start(x_sb[i][:], x[i * P : (i + 1) * P, :])
+        for s in range(IN_BLOCKS + STAGES):
+            if s < IN_BLOCKS:
+                nc.sync.dma_start(x_sb[s][:], x[s * P : (s + 1) * P, :])
             for k in range(ORDERS):
-                first_row = k * C_IN + i * P
-                nc.sync.dma_start(w_sb[k][:, i, :], w[first_row : first_row + P, :])
+                i = s - FEED_LAG[k]
+                if 0 <= i < IN_BLOCKS:
+                    first_row = k * C_IN + i * P
+                    nc.sync.dma_start(w_sb[k][:, i, :], w[first_row : first_row + P, :])
         offsets = held.tile([P, N // 16], U16, name="offsets")
         nc.sync.dma_start(offsets[:], offs)
         bias = held.tile([P, OUT_BLOCKS], F32, name="bias")
@@ -153,14 +157,14 @@ def tile_chebconv2d_b_kernel(tc, x, adj, w, b, base, offs, out):
         for s in range(IN_BLOCKS + STAGES):
             if s < IN_BLOCKS:
                 turn_x(s)
-                feed_early(0, s)
+                feed_early(0, s - FEED_LAG[0])
             if 0 <= s - 1 < IN_BLOCKS:
                 first_order(s - 1)
             if 0 <= s - 2 < IN_BLOCKS:
-                feed_early(1, s - 2)
+                feed_early(1, s - FEED_LAG[1])
                 second_order(s - 2)
             if 0 <= s - 3 < IN_BLOCKS:
-                feed_early(2, s - 3)
+                feed_early(2, s - FEED_LAG[2])
         for o in range(EARLY_OUT_BLOCKS):
             place(o, early[o])
 

@@ -15,8 +15,9 @@ BANKS = 8
 HALVES = N // BANK
 ROWS_PER_BANK = BANK // P
 EARLY_OUT_BLOCKS = 2
-STAGES = 3
-FEED_LAG = (0, 2, 3)
+L_LAG = 3
+FEED_LAG = (0, L_LAG + 1, L_LAG + 2)
+STEPS = IN_BLOCKS + FEED_LAG[2]
 WARM_UP = 5
 
 FLOPS = 2 * ORDERS * C_IN * C_OUT * N + 2 * (2 * P * P * C_IN * ROWS)
@@ -30,10 +31,9 @@ def tile_chebconv2d_b_kernel(tc, x, adj, w, b, base, offs, out):
         tc.psum_pool(name="psum", bufs=BANKS) as psum,
     ):
         adj_sb = held.tile([P, P], F32, name="adj_sb")
-        nc.sync.dma_start(adj_sb[:], adj)
         x_sb = [held.tile([P, N], BF16, name=f"x{i}") for i in range(IN_BLOCKS)]
         w_sb = [held.tile([P, IN_BLOCKS, C_OUT], BF16, name=f"w{k}") for k in range(ORDERS)]
-        for s in range(IN_BLOCKS + STAGES):
+        for s in range(STEPS):
             if s < IN_BLOCKS:
                 nc.sync.dma_start(x_sb[s][:], x[s * P : (s + 1) * P, :])
             for k in range(ORDERS):
@@ -41,6 +41,8 @@ def tile_chebconv2d_b_kernel(tc, x, adj, w, b, base, offs, out):
                 if 0 <= i < IN_BLOCKS:
                     first_row = k * C_IN + i * P
                     nc.sync.dma_start(w_sb[k][:, i, :], w[first_row : first_row + P, :])
+            if s == 0:
+                nc.sync.dma_start(adj_sb[:], adj)
         offsets = held.tile([P, N // 16], U16, name="offsets")
         nc.sync.dma_start(offsets[:], offs)
         bias = held.tile([P, OUT_BLOCKS], F32, name="bias")
@@ -65,26 +67,27 @@ def tile_chebconv2d_b_kernel(tc, x, adj, w, b, base, offs, out):
         make_identity(nc, identity_bf16[:])
         ones = held.tile([P, 1], F32, name="ones")
         nc.vector.memset(ones[:], 1.0)
-
         off_diagonal = held.tile([P, P], F32, name="off_diagonal")
         nc.vector.tensor_scalar(off_diagonal[:], identity_f32[:], -1.0, 1.0, op0=MULT, op1=ADD)
-        a_sb = held.tile([P, P], F32, name="a_sb")
-        nc.vector.tensor_tensor(a_sb[:], adj_sb[:], off_diagonal[:], MULT)
-        row_sums = held.tile([P, 1], F32, name="row_sums")
-        nc.vector.reduce_sum(row_sums[:], a_sb[:], axis=mybir.AxisListType.X)
-        col_sums = psum.tile([P, BANK], F32, tag="bank", name="col_sums")
-        nc.tensor.matmul(col_sums[:, 0:1], lhsT=a_sb[:], rhs=ones[:], start=True, stop=True)
-        roots = held.tile([P, 2], F32, name="roots")
-        nc.scalar.sqrt(roots[:, 0:1], col_sums[:, 0:1])
-        nc.scalar.sqrt(roots[:, 1:2], row_sums[:])
-        inverse_roots = held.tile([P, 2], F32, name="inverse_roots")
-        nc.vector.reciprocal(inverse_roots[:], roots[:])
-        a_scaled = held.tile([P, P], F32, name="a_scaled")
-        nc.vector.tensor_scalar_mul(a_scaled[:], a_sb[:], inverse_roots[:, 0:1])
-        a_turned = psum.tile([P, BANK], F32, tag="bank", name="a_turned")
-        nc.tensor.transpose(a_turned[:, 0:P], a_scaled[:], identity_f32[:])
         lt = held.tile([P, P], BF16, name="lt")
-        nc.vector.tensor_scalar_mul(lt[:], a_turned[:, 0:P], inverse_roots[:, 1:2])
+
+        def make_lt():
+            a_sb = held.tile([P, P], F32, name="a_sb")
+            nc.vector.tensor_tensor(a_sb[:], adj_sb[:], off_diagonal[:], MULT)
+            row_sums = held.tile([P, 1], F32, name="row_sums")
+            nc.vector.reduce_sum(row_sums[:], a_sb[:], axis=mybir.AxisListType.X)
+            col_sums = psum.tile([P, BANK], F32, tag="bank", name="col_sums")
+            nc.tensor.matmul(col_sums[:, 0:1], lhsT=a_sb[:], rhs=ones[:], start=True, stop=True)
+            roots = held.tile([P, 2], F32, name="roots")
+            nc.scalar.sqrt(roots[:, 0:1], col_sums[:, 0:1])
+            nc.scalar.sqrt(roots[:, 1:2], row_sums[:])
+            inverse_roots = held.tile([P, 2], F32, name="inverse_roots")
+            nc.vector.reciprocal(inverse_roots[:], roots[:])
+            a_scaled = held.tile([P, P], F32, name="a_scaled")
+            nc.vector.tensor_scalar_mul(a_scaled[:], a_sb[:], inverse_roots[:, 0:1])
+            a_turned = psum.tile([P, BANK], F32, tag="bank", name="a_turned")
+            nc.tensor.transpose(a_turned[:, 0:P], a_scaled[:], identity_f32[:])
+            nc.vector.tensor_scalar_mul(lt[:], a_turned[:, 0:P], inverse_roots[:, 1:2])
 
         xt = [held.tile([P, N], BF16, name=f"xt{i}") for i in range(IN_BLOCKS)]
         t1t = [held.tile([P, N], BF16, name=f"t1t{i}") for i in range(IN_BLOCKS)]
@@ -154,16 +157,18 @@ def tile_chebconv2d_b_kernel(tc, x, adj, w, b, base, offs, out):
                 for h in range(HALVES):
                     add_to_y(early[o][h], o, h, k, i)
 
-        for s in range(IN_BLOCKS + STAGES):
+        for s in range(STEPS):
             if s < IN_BLOCKS:
                 turn_x(s)
                 feed_early(0, s - FEED_LAG[0])
-            if 0 <= s - 1 < IN_BLOCKS:
-                first_order(s - 1)
-            if 0 <= s - 2 < IN_BLOCKS:
+            if s == 0:
+                make_lt()
+            if 0 <= s - L_LAG < IN_BLOCKS:
+                first_order(s - L_LAG)
+            if 0 <= s - FEED_LAG[1] < IN_BLOCKS:
                 feed_early(1, s - FEED_LAG[1])
-                second_order(s - 2)
-            if 0 <= s - 3 < IN_BLOCKS:
+                second_order(s - FEED_LAG[1])
+            if 0 <= s - FEED_LAG[2] < IN_BLOCKS:
                 feed_early(2, s - FEED_LAG[2])
         for o in range(EARLY_OUT_BLOCKS):
             place(o, early[o])

@@ -16,9 +16,9 @@ HALVES = N // BANK
 ROWS_PER_BANK = BANK // P
 EARLY_OUT_BLOCKS = 2
 L_LAG = 3
-FEED_LAG = (0, L_LAG + 1, L_LAG + 2)
+FEED_LAG = (0, L_LAG + 2, L_LAG + 2)
 STEPS = IN_BLOCKS + FEED_LAG[2]
-WARM_UP = 5
+WARM_UP = 3
 
 FLOPS = 2 * ORDERS * C_IN * C_OUT * N + 2 * (2 * P * P * C_IN * ROWS)
 
@@ -108,13 +108,13 @@ def tile_chebconv2d_b_kernel(tc, x, adj, w, b, base, offs, out):
                 half = slice(h * BANK, (h + 1) * BANK)
                 nc.tensor.matmul(t1t_ps[:, half], lhsT=lt[:], rhs=xt[i][:, half], start=True, stop=True)
             nc.scalar.copy(t1t[i][:], t1t_ps[:])
+
+        def second_order(i):
             t1_ps = psum.tile([P, N], BF16, tag="bank", name="t1_ps")
             for r in range(ROWS):
                 row = slice(r * P, (r + 1) * P)
-                nc.tensor.matmul(t1_ps[:, row], lhsT=xt[i][:, row], rhs=lt[:], start=True, stop=True)
+                nc.tensor.transpose(t1_ps[:, row], t1t[i][:, row], identity_bf16[:])
             nc.scalar.copy(t1[i][:], t1_ps[:])
-
-        def second_order(i):
             for h in range(HALVES):
                 half = slice(h * BANK, (h + 1) * BANK)
                 t2_ps = psum.tile([P, BANK], F32, tag="bank", name="t2_ps")
@@ -165,10 +165,10 @@ def tile_chebconv2d_b_kernel(tc, x, adj, w, b, base, offs, out):
                 make_lt()
             if 0 <= s - L_LAG < IN_BLOCKS:
                 first_order(s - L_LAG)
+            if 0 <= s - L_LAG - 1 < IN_BLOCKS:
+                second_order(s - L_LAG - 1)
             if 0 <= s - FEED_LAG[1] < IN_BLOCKS:
                 feed_early(1, s - FEED_LAG[1])
-                second_order(s - FEED_LAG[1])
-            if 0 <= s - FEED_LAG[2] < IN_BLOCKS:
                 feed_early(2, s - FEED_LAG[2])
         for o in range(EARLY_OUT_BLOCKS):
             place(o, early[o])

@@ -111,25 +111,17 @@ def tile_chebconv2d_b_kernel(tc, x, adj, w, b, base, offs, out):
 
         def second_order(i):
             t1_ps = psum.tile([P, N], BF16, tag="bank", name="t1_ps")
-            for r in range(ROWS):
-                row = slice(r * P, (r + 1) * P)
-                nc.tensor.transpose(t1_ps[:, row], t1t[i][:, row], identity_bf16[:])
-            nc.scalar.copy(t1[i][:], t1_ps[:])
             for h in range(HALVES):
                 half = slice(h * BANK, (h + 1) * BANK)
                 t2_ps = psum.tile([P, BANK], F32, tag="bank", name="t2_ps")
                 for q in range(ROWS_PER_BANK):
-                    r = h * ROWS_PER_BANK + q
-                    nc.tensor.matmul(
-                        t2_ps[:, q * P : (q + 1) * P],
-                        lhsT=t1t[i][:, r * P : (r + 1) * P],
-                        rhs=lt[:],
-                        start=True,
-                        stop=True,
-                    )
+                    row = slice((h * ROWS_PER_BANK + q) * P, (h * ROWS_PER_BANK + q + 1) * P)
+                    nc.tensor.transpose(t1_ps[:, row], t1t[i][:, row], identity_bf16[:])
+                    nc.tensor.matmul(t2_ps[:, q * P : (q + 1) * P], lhsT=t1t[i][:, row], rhs=lt[:], start=True, stop=True)
                 nc.vector.scalar_tensor_tensor(
                     t2[i][:, half], in0=t2_ps[:], scalar=2.0, in1=x_sb[i][:, half], op0=MULT, op1=SUBTRACT
                 )
+            nc.scalar.copy(t1[i][:], t1_ps[:])
 
         def add_to_y(y_ps, o, h, k, i):
             nc.tensor.matmul(

@@ -15,7 +15,7 @@ BANKS = 8
 HALVES = N // BANK
 ROWS_PER_BANK = BANK // P
 EARLY_OUT_BLOCKS = 2
-L_LAG = 3
+L_LAG = 4
 FEED_LAG = (0, L_LAG + 2, L_LAG + 2)
 STEPS = IN_BLOCKS + FEED_LAG[2]
 WARM_UP = 3
@@ -70,8 +70,10 @@ def tile_chebconv2d_b_kernel(tc, x, adj, w, b, base, offs, out):
         off_diagonal = held.tile([P, P], F32, name="off_diagonal")
         nc.vector.tensor_scalar(off_diagonal[:], identity_f32[:], -1.0, 1.0, op0=MULT, op1=ADD)
         lt = held.tile([P, P], BF16, name="lt")
+        inverse_roots = held.tile([P, 2], F32, name="inverse_roots")
+        a_scaled = held.tile([P, P], F32, name="a_scaled")
 
-        def make_lt():
+        def scale_rows_of_a():
             a_sb = held.tile([P, P], F32, name="a_sb")
             nc.vector.tensor_tensor(a_sb[:], adj_sb[:], off_diagonal[:], MULT)
             row_sums = held.tile([P, 1], F32, name="row_sums")
@@ -81,10 +83,10 @@ def tile_chebconv2d_b_kernel(tc, x, adj, w, b, base, offs, out):
             roots = held.tile([P, 2], F32, name="roots")
             nc.scalar.sqrt(roots[:, 0:1], col_sums[:, 0:1])
             nc.scalar.sqrt(roots[:, 1:2], row_sums[:])
-            inverse_roots = held.tile([P, 2], F32, name="inverse_roots")
             nc.vector.reciprocal(inverse_roots[:], roots[:])
-            a_scaled = held.tile([P, P], F32, name="a_scaled")
             nc.vector.tensor_scalar_mul(a_scaled[:], a_sb[:], inverse_roots[:, 0:1])
+
+        def turn_and_scale_columns_of_a():
             a_turned = psum.tile([P, BANK], F32, tag="bank", name="a_turned")
             nc.tensor.transpose(a_turned[:, 0:P], a_scaled[:], identity_f32[:])
             nc.vector.tensor_scalar_mul(lt[:], a_turned[:, 0:P], inverse_roots[:, 1:2])
@@ -153,8 +155,10 @@ def tile_chebconv2d_b_kernel(tc, x, adj, w, b, base, offs, out):
             if s < IN_BLOCKS:
                 turn_x(s)
                 feed_early(0, s - FEED_LAG[0])
-            if s == 0:
-                make_lt()
+            if s == 1:
+                scale_rows_of_a()
+            if s == L_LAG - 1:
+                turn_and_scale_columns_of_a()
             if 0 <= s - L_LAG < IN_BLOCKS:
                 first_order(s - L_LAG)
             if 0 <= s - L_LAG - 1 < IN_BLOCKS:

@@ -13,12 +13,14 @@ OUT_BLOCKS = C_OUT // P
 BANK = 512
 BANKS = 8
 HALVES = N // BANK
+HALF_COLUMNS = (slice(0, BANK), slice(BANK, N))
+LAST_COLUMNS = (slice(0, BANK), slice(BANK, N - BANK // 2), slice(N - BANK // 2, N))
 ROWS_PER_BANK = BANK // P
 EARLY_OUT_BLOCKS = 2
 L_LAG = 4
 FEED_LAG = (0, L_LAG + 2, L_LAG + 2)
 STEPS = IN_BLOCKS + FEED_LAG[2]
-WARM_UP = 3
+WARM_UP = 16
 
 FLOPS = 2 * ORDERS * C_IN * C_OUT * N + 2 * (2 * P * P * C_IN * ROWS)
 
@@ -30,6 +32,12 @@ def tile_chebconv2d_b_kernel(tc, x, adj, w, b, base, offs, out):
         tc.tile_pool(name="dense", bufs=2) as dense,
         tc.psum_pool(name="psum", bufs=BANKS) as psum,
     ):
+        zeros = held.tile([P, P], BF16, name="zeros")
+        nc.gpsimd.memset(zeros[:], 0.0)
+        warm_ps = psum.tile([P, BANK], F32, tag="bank", name="warm_ps")
+        for repeat in range(WARM_UP):
+            nc.tensor.matmul(warm_ps[:, 0:P], lhsT=zeros[:], rhs=zeros[:], start=True, stop=True)
+
         adj_sb = held.tile([P, P], F32, name="adj_sb")
         x_sb = [held.tile([P, N], BF16, name=f"x{i}") for i in range(IN_BLOCKS)]
         w_sb = [held.tile([P, IN_BLOCKS, C_OUT], BF16, name=f"w{k}") for k in range(ORDERS)]
@@ -54,12 +62,6 @@ def tile_chebconv2d_b_kernel(tc, x, adj, w, b, base, offs, out):
         bias_wide = [held.tile([P, N], F32, name=f"bias_wide{o}") for o in range(OUT_BLOCKS)]
         for o in range(OUT_BLOCKS):
             nc.gpsimd.tensor_copy(bias_wide[o][:], bias[:, o : o + 1].to_broadcast([P, N]))
-
-        zeros = held.tile([P, BANK], BF16, name="zeros")
-        nc.vector.memset(zeros[:], 0.0)
-        warm_ps = psum.tile([P, BANK], F32, tag="bank", name="warm_ps")
-        for repeat in range(WARM_UP):
-            nc.tensor.matmul(warm_ps[:], lhsT=zeros[:, 0:P], rhs=zeros[:], start=True, stop=True)
 
         identity_f32 = held.tile([P, P], F32, name="identity_f32")
         make_identity(nc, identity_f32[:])
@@ -109,7 +111,7 @@ def tile_chebconv2d_b_kernel(tc, x, adj, w, b, base, offs, out):
             for h in range(HALVES):
                 half = slice(h * BANK, (h + 1) * BANK)
                 nc.tensor.matmul(t1t_ps[:, half], lhsT=lt[:], rhs=xt[i][:, half], start=True, stop=True)
-            nc.scalar.copy(t1t[i][:], t1t_ps[:])
+            nc.vector.tensor_copy(t1t[i][:], t1t_ps[:])
 
         def second_order(i):
             t1_ps = psum.tile([P, N], BF16, tag="bank", name="t1_ps")
@@ -125,19 +127,20 @@ def tile_chebconv2d_b_kernel(tc, x, adj, w, b, base, offs, out):
                 )
             nc.scalar.copy(t1[i][:], t1_ps[:])
 
-        def add_to_y(y_ps, o, h, k, i):
+        def add_to_y(y_ps, o, columns, k, i):
             nc.tensor.matmul(
-                y_ps[:],
+                y_ps[:, 0 : columns.stop - columns.start],
                 lhsT=w_sb[k][:, i, o * P : (o + 1) * P],
-                rhs=terms[k][i][:, h * BANK : (h + 1) * BANK],
+                rhs=terms[k][i][:, columns],
                 start=(k == 0 and i == 0),
                 stop=(k == ORDERS - 1 and i == IN_BLOCKS - 1),
             )
 
-        def place(o, y_halves):
+        def place(o, groups, y_groups):
             y_sb = dense.tile([P, N], F32, name="y_sb")
-            for h in range(HALVES):
-                nc.scalar.copy(y_sb[:, h * BANK : (h + 1) * BANK], y_halves[h][:])
+            for columns, y_ps in zip(groups, y_groups):
+                copy = nc.vector.tensor_copy if columns.stop == N else nc.scalar.copy
+                copy(y_sb[:, columns], y_ps[:, 0 : columns.stop - columns.start])
             nc.vector.tensor_tensor(window[o][:].indirect(offsets[:]), y_sb[:], bias_wide[o][:], ADD)
             nc.sync.dma_start(out[o * P : (o + 1) * P, :], window[o][:])
 
@@ -149,7 +152,7 @@ def tile_chebconv2d_b_kernel(tc, x, adj, w, b, base, offs, out):
         def feed_early(k, i):
             for o in range(EARLY_OUT_BLOCKS):
                 for h in range(HALVES):
-                    add_to_y(early[o][h], o, h, k, i)
+                    add_to_y(early[o][h], o, HALF_COLUMNS[h], k, i)
 
         for s in range(STEPS):
             if s < IN_BLOCKS:
@@ -167,14 +170,15 @@ def tile_chebconv2d_b_kernel(tc, x, adj, w, b, base, offs, out):
                 feed_early(1, s - FEED_LAG[1])
                 feed_early(2, s - FEED_LAG[2])
         for o in range(EARLY_OUT_BLOCKS):
-            place(o, early[o])
+            place(o, HALF_COLUMNS, early[o])
 
         for o in range(EARLY_OUT_BLOCKS, OUT_BLOCKS):
-            y_halves = []
-            for h in range(HALVES):
+            groups = HALF_COLUMNS if o < OUT_BLOCKS - 1 else LAST_COLUMNS
+            y_groups = []
+            for columns in groups:
                 y_ps = psum.tile([P, BANK], F32, tag="bank", name="y_ps")
                 for k in range(ORDERS):
                     for i in range(IN_BLOCKS):
-                        add_to_y(y_ps, o, h, k, i)
-                y_halves.append(y_ps)
-            place(o, y_halves)
+                        add_to_y(y_ps, o, columns, k, i)
+                y_groups.append(y_ps)
+            place(o, groups, y_groups)

@@ -41,12 +41,15 @@ def tile_chebconv2d_b_kernel(tc, x, adj, w, b, base, offs, out):
         adj_sb = held.tile([P, P], F32, name="adj_sb")
         x_sb = [held.tile([P, N], BF16, name=f"x{i}") for i in range(IN_BLOCKS)]
         w_sb = [held.tile([P, IN_BLOCKS, C_OUT], BF16, name=f"w{k}") for k in range(ORDERS)]
+        nc.sync.dma_start(x_sb[0][:, HALF_COLUMNS[0]], x[0:P, HALF_COLUMNS[0]])
+        nc.sync.dma_start(w_sb[0][:, 0, :], w[0:P, :])
+        nc.sync.dma_start(x_sb[0][:, HALF_COLUMNS[1]], x[0:P, HALF_COLUMNS[1]])
         for s in range(STEPS):
-            if s < IN_BLOCKS:
+            if 0 < s < IN_BLOCKS:
                 nc.sync.dma_start(x_sb[s][:], x[s * P : (s + 1) * P, :])
             for k in range(ORDERS):
                 i = s - FEED_LAG[k]
-                if 0 <= i < IN_BLOCKS:
+                if 0 <= i < IN_BLOCKS and s > 0:
                     first_row = k * C_IN + i * P
                     nc.sync.dma_start(w_sb[k][:, i, :], w[first_row : first_row + P, :])
             if s == 0:
@@ -99,11 +102,13 @@ def tile_chebconv2d_b_kernel(tc, x, adj, w, b, base, offs, out):
         t2 = [held.tile([P, N], BF16, name=f"t2_{i}") for i in range(IN_BLOCKS)]
         terms = [x_sb, t1, t2]
 
-        def turn_x(i):
+        def turn_x_and_feed_it(i):
             xt_ps = psum.tile([P, N], BF16, tag="bank", name="xt_ps")
-            for r in range(ROWS):
-                row = slice(r * P, (r + 1) * P)
-                nc.tensor.transpose(xt_ps[:, row], x_sb[i][:, row], identity_bf16[:])
+            for h in range(HALVES):
+                for r in range(h * ROWS_PER_BANK, (h + 1) * ROWS_PER_BANK):
+                    row = slice(r * P, (r + 1) * P)
+                    nc.tensor.transpose(xt_ps[:, row], x_sb[i][:, row], identity_bf16[:])
+                feed_early(0, i, h)
             nc.vector.tensor_copy(xt[i][:], xt_ps[:])
 
         def first_order(i):
@@ -149,15 +154,13 @@ def tile_chebconv2d_b_kernel(tc, x, adj, w, b, base, offs, out):
             for o in range(EARLY_OUT_BLOCKS)
         ]
 
-        def feed_early(k, i):
+        def feed_early(k, i, h):
             for o in range(EARLY_OUT_BLOCKS):
-                for h in range(HALVES):
-                    add_to_y(early[o][h], o, HALF_COLUMNS[h], k, i)
+                add_to_y(early[o][h], o, HALF_COLUMNS[h], k, i)
 
         for s in range(STEPS):
             if s < IN_BLOCKS:
-                turn_x(s)
-                feed_early(0, s - FEED_LAG[0])
+                turn_x_and_feed_it(s)
             if s == 1:
                 scale_rows_of_a()
             if s == L_LAG - 1:
@@ -167,8 +170,9 @@ def tile_chebconv2d_b_kernel(tc, x, adj, w, b, base, offs, out):
             if 0 <= s - L_LAG - 1 < IN_BLOCKS:
                 second_order(s - L_LAG - 1)
             if 0 <= s - FEED_LAG[1] < IN_BLOCKS:
-                feed_early(1, s - FEED_LAG[1])
-                feed_early(2, s - FEED_LAG[2])
+                for k in (1, 2):
+                    for h in range(HALVES):
+                        feed_early(k, s - FEED_LAG[k], h)
         for o in range(EARLY_OUT_BLOCKS):
             place(o, HALF_COLUMNS, early[o])
 

@@ -14,13 +14,13 @@ BANK = 512
 BANKS = 8
 HALVES = N // BANK
 HALF_COLUMNS = (slice(0, BANK), slice(BANK, N))
-LAST_COLUMNS = (slice(0, BANK), slice(BANK, N - BANK // 2), slice(N - BANK // 2, N))
+LAST_COLUMNS = (slice(0, BANK), slice(BANK, N - P), slice(N - P, N))
 ROWS_PER_BANK = BANK // P
 EARLY_OUT_BLOCKS = 2
 L_LAG = 4
 FEED_LAG = (0, L_LAG + 2, L_LAG + 2)
 STEPS = IN_BLOCKS + FEED_LAG[2]
-WARM_UP = 16
+WARM_UP = 13
 
 FLOPS = 2 * ORDERS * C_IN * C_OUT * N + 2 * (2 * P * P * C_IN * ROWS)
 
@@ -104,11 +104,14 @@ def tile_chebconv2d_b_kernel(tc, x, adj, w, b, base, offs, out):
 
         def turn_x_and_feed_it(i):
             xt_ps = psum.tile([P, N], BF16, tag="bank", name="xt_ps")
+            share = ROWS_PER_BANK // EARLY_OUT_BLOCKS
             for h in range(HALVES):
-                for r in range(h * ROWS_PER_BANK, (h + 1) * ROWS_PER_BANK):
-                    row = slice(r * P, (r + 1) * P)
-                    nc.tensor.transpose(xt_ps[:, row], x_sb[i][:, row], identity_bf16[:])
-                feed_early(0, i, h)
+                for o in range(EARLY_OUT_BLOCKS):
+                    first = h * ROWS_PER_BANK + o * share
+                    for r in range(first, first + share):
+                        row = slice(r * P, (r + 1) * P)
+                        nc.tensor.transpose(xt_ps[:, row], x_sb[i][:, row], identity_bf16[:])
+                    add_to_y(early[o][h], o, HALF_COLUMNS[h], 0, i)
             nc.vector.tensor_copy(xt[i][:], xt_ps[:])
 
         def first_order(i):

import concourse.mybir as mybir
from concourse.masks import make_identity

BF16, F32, U16 = mybir.dt.bfloat16, mybir.dt.float32, mybir.dt.uint16
ADD, MULT, SUBTRACT = mybir.AluOpType.add, mybir.AluOpType.mult, mybir.AluOpType.subtract

P = 128
ROWS = 8
N = ROWS * P
C_IN, ORDERS, C_OUT, STORE = 1024, 3, 512, 2048
IN_BLOCKS = C_IN // P
OUT_BLOCKS = C_OUT // P
BANK = 512
BANKS = 8
HALVES = N // BANK
HALF_COLUMNS = (slice(0, BANK), slice(BANK, N))
LAST_COLUMNS = (slice(0, BANK), slice(BANK, N - P), slice(N - P, N))
ROWS_PER_BANK = BANK // P
EARLY_OUT_BLOCKS = 2
L_LAG = 4
FEED_LAG = (0, L_LAG + 2, L_LAG + 2)
STEPS = IN_BLOCKS + FEED_LAG[2]
WARM_UP = 13

FLOPS = 2 * ORDERS * C_IN * C_OUT * N + 2 * (2 * P * P * C_IN * ROWS)


def tile_chebconv2d_b_kernel(tc, x, adj, w, b, base, offs, out):
    nc = tc.nc
    with (
        tc.tile_pool(name="held", bufs=1) as held,
        tc.tile_pool(name="dense", bufs=2) as dense,
        tc.psum_pool(name="psum", bufs=BANKS) as psum,
    ):
        zeros = held.tile([P, P], BF16, name="zeros")
        nc.gpsimd.memset(zeros[:], 0.0)
        warm_ps = psum.tile([P, BANK], F32, tag="bank", name="warm_ps")
        for repeat in range(WARM_UP):
            nc.tensor.matmul(warm_ps[:, 0:P], lhsT=zeros[:], rhs=zeros[:], start=True, stop=True)

        adj_sb = held.tile([P, P], F32, name="adj_sb")
        x_sb = [held.tile([P, N], BF16, name=f"x{i}") for i in range(IN_BLOCKS)]
        w_sb = [held.tile([P, IN_BLOCKS, C_OUT], BF16, name=f"w{k}") for k in range(ORDERS)]
        nc.sync.dma_start(x_sb[0][:, HALF_COLUMNS[0]], x[0:P, HALF_COLUMNS[0]])
        nc.sync.dma_start(w_sb[0][:, 0, :], w[0:P, :])
        nc.sync.dma_start(x_sb[0][:, HALF_COLUMNS[1]], x[0:P, HALF_COLUMNS[1]])
        for s in range(STEPS):
            if 0 < s < IN_BLOCKS:
                nc.sync.dma_start(x_sb[s][:], x[s * P : (s + 1) * P, :])
            for k in range(ORDERS):
                i = s - FEED_LAG[k]
                if 0 <= i < IN_BLOCKS and s > 0:
                    first_row = k * C_IN + i * P
                    nc.sync.dma_start(w_sb[k][:, i, :], w[first_row : first_row + P, :])
            if s == 0:
                nc.sync.dma_start(adj_sb[:], adj)
        offsets = held.tile([P, N // 16], U16, name="offsets")
        nc.sync.dma_start(offsets[:], offs)
        bias = held.tile([P, OUT_BLOCKS], F32, name="bias")
        with nc.allow_non_contiguous_dma(reason="512 floats, one to a partition and block"):
            nc.sync.dma_start(bias[:], b.rearrange("(o p) one -> p (o one)", p=P))
        window = [held.tile([P, STORE], F32, name=f"window{o}") for o in range(OUT_BLOCKS)]
        for o in range(OUT_BLOCKS):
            nc.sync.dma_start(window[o][:], base[o * P : (o + 1) * P, :])
        bias_wide = [held.tile([P, N], F32, name=f"bias_wide{o}") for o in range(OUT_BLOCKS)]
        for o in range(OUT_BLOCKS):
            nc.gpsimd.tensor_copy(bias_wide[o][:], bias[:, o : o + 1].to_broadcast([P, N]))

        identity_f32 = held.tile([P, P], F32, name="identity_f32")
        make_identity(nc, identity_f32[:])
        identity_bf16 = held.tile([P, P], BF16, name="identity_bf16")
        make_identity(nc, identity_bf16[:])
        ones = held.tile([P, 1], F32, name="ones")
        nc.vector.memset(ones[:], 1.0)
        off_diagonal = held.tile([P, P], F32, name="off_diagonal")
        nc.vector.tensor_scalar(off_diagonal[:], identity_f32[:], -1.0, 1.0, op0=MULT, op1=ADD)
        lt = held.tile([P, P], BF16, name="lt")
        inverse_roots = held.tile([P, 2], F32, name="inverse_roots")
        a_scaled = held.tile([P, P], F32, name="a_scaled")

        def scale_rows_of_a():
            a_sb = held.tile([P, P], F32, name="a_sb")
            nc.vector.tensor_tensor(a_sb[:], adj_sb[:], off_diagonal[:], MULT)
            row_sums = held.tile([P, 1], F32, name="row_sums")
            nc.vector.reduce_sum(row_sums[:], a_sb[:], axis=mybir.AxisListType.X)
            col_sums = psum.tile([P, BANK], F32, tag="bank", name="col_sums")
            nc.tensor.matmul(col_sums[:, 0:1], lhsT=a_sb[:], rhs=ones[:], start=True, stop=True)
            roots = held.tile([P, 2], F32, name="roots")
            nc.scalar.sqrt(roots[:, 0:1], col_sums[:, 0:1])
            nc.scalar.sqrt(roots[:, 1:2], row_sums[:])
            nc.vector.reciprocal(inverse_roots[:], roots[:])
            nc.vector.tensor_scalar_mul(a_scaled[:], a_sb[:], inverse_roots[:, 0:1])

        def turn_and_scale_columns_of_a():
            a_turned = psum.tile([P, BANK], F32, tag="bank", name="a_turned")
            nc.tensor.transpose(a_turned[:, 0:P], a_scaled[:], identity_f32[:])
            nc.vector.tensor_scalar_mul(lt[:], a_turned[:, 0:P], inverse_roots[:, 1:2])

        xt = [held.tile([P, N], BF16, name=f"xt{i}") for i in range(IN_BLOCKS)]
        t1t = [held.tile([P, N], BF16, name=f"t1t{i}") for i in range(IN_BLOCKS)]
        t1 = [held.tile([P, N], BF16, name=f"t1_{i}") for i in range(IN_BLOCKS)]
        t2 = [held.tile([P, N], BF16, name=f"t2_{i}") for i in range(IN_BLOCKS)]
        terms = [x_sb, t1, t2]

        def turn_x_and_feed_it(i):
            xt_ps = psum.tile([P, N], BF16, tag="bank", name="xt_ps")
            share = ROWS_PER_BANK // EARLY_OUT_BLOCKS
            for h in range(HALVES):
                for o in range(EARLY_OUT_BLOCKS):
                    first = h * ROWS_PER_BANK + o * share
                    for r in range(first, first + share):
                        row = slice(r * P, (r + 1) * P)
                        nc.tensor.transpose(xt_ps[:, row], x_sb[i][:, row], identity_bf16[:])
                    add_to_y(early[o][h], o, HALF_COLUMNS[h], 0, i)
            nc.vector.tensor_copy(xt[i][:], xt_ps[:])

        def first_order(i):
            t1t_ps = psum.tile([P, N], BF16, tag="bank", name="t1t_ps")
            for h in range(HALVES):
                half = slice(h * BANK, (h + 1) * BANK)
                nc.tensor.matmul(t1t_ps[:, half], lhsT=lt[:], rhs=xt[i][:, half], start=True, stop=True)
            nc.vector.tensor_copy(t1t[i][:], t1t_ps[:])

        def second_order(i):
            t1_ps = psum.tile([P, N], BF16, tag="bank", name="t1_ps")
            for h in range(HALVES):
                half = slice(h * BANK, (h + 1) * BANK)
                t2_ps = psum.tile([P, BANK], F32, tag="bank", name="t2_ps")
                for q in range(ROWS_PER_BANK):
                    row = slice((h * ROWS_PER_BANK + q) * P, (h * ROWS_PER_BANK + q + 1) * P)
                    nc.tensor.transpose(t1_ps[:, row], t1t[i][:, row], identity_bf16[:])
                    nc.tensor.matmul(t2_ps[:, q * P : (q + 1) * P], lhsT=t1t[i][:, row], rhs=lt[:], start=True, stop=True)
                nc.vector.scalar_tensor_tensor(
                    t2[i][:, half], in0=t2_ps[:], scalar=2.0, in1=x_sb[i][:, half], op0=MULT, op1=SUBTRACT
                )
            nc.scalar.copy(t1[i][:], t1_ps[:])

        def add_to_y(y_ps, o, columns, k, i):
            nc.tensor.matmul(
                y_ps[:, 0 : columns.stop - columns.start],
                lhsT=w_sb[k][:, i, o * P : (o + 1) * P],
                rhs=terms[k][i][:, columns],
                start=(k == 0 and i == 0),
                stop=(k == ORDERS - 1 and i == IN_BLOCKS - 1),
            )

        def place(o, groups, y_groups):
            y_sb = dense.tile([P, N], F32, name="y_sb")
            for columns, y_ps in zip(groups, y_groups):
                copy = nc.vector.tensor_copy if columns.stop == N else nc.scalar.copy
                copy(y_sb[:, columns], y_ps[:, 0 : columns.stop - columns.start])
            nc.vector.tensor_tensor(window[o][:].indirect(offsets[:]), y_sb[:], bias_wide[o][:], ADD)
            nc.sync.dma_start(out[o * P : (o + 1) * P, :], window[o][:])

        early = [
            [psum.tile([P, BANK], F32, tag="bank", name=f"y_ps{o}_{h}") for h in range(HALVES)]
            for o in range(EARLY_OUT_BLOCKS)
        ]

        def feed_early(k, i, h):
            for o in range(EARLY_OUT_BLOCKS):
                add_to_y(early[o][h], o, HALF_COLUMNS[h], k, i)

        for s in range(STEPS):
            if s < IN_BLOCKS:
                turn_x_and_feed_it(s)
            if s == 1:
                scale_rows_of_a()
            if s == L_LAG - 1:
                turn_and_scale_columns_of_a()
            if 0 <= s - L_LAG < IN_BLOCKS:
                first_order(s - L_LAG)
            if 0 <= s - L_LAG - 1 < IN_BLOCKS:
                second_order(s - L_LAG - 1)
            if 0 <= s - FEED_LAG[1] < IN_BLOCKS:
                for k in (1, 2):
                    for h in range(HALVES):
                        feed_early(k, s - FEED_LAG[k], h)
        for o in range(EARLY_OUT_BLOCKS):
            place(o, HALF_COLUMNS, early[o])

        for o in range(EARLY_OUT_BLOCKS, OUT_BLOCKS):
            groups = HALF_COLUMNS if o < OUT_BLOCKS - 1 else LAST_COLUMNS
            y_groups = []
            for columns in groups:
                y_ps = psum.tile([P, BANK], F32, tag="bank", name="y_ps")
                for k in range(ORDERS):
                    for i in range(IN_BLOCKS):
                        add_to_y(y_ps, o, columns, k, i)
                y_groups.append(y_ps)
            place(o, groups, y_groups)
